import numpy as np
import ml_dtypes


def mxq(x, axis, fmt="e4m3"):
    dtype, down = {"e4m3": (ml_dtypes.float8_e4m3fn, 7), "e5m2": (ml_dtypes.float8_e5m2, 14)}[fmt]
    v = np.moveaxis(np.asarray(x, np.float32).astype(ml_dtypes.bfloat16).astype(np.float64), axis, -1)
    blocks = v.reshape(v.shape[:-1] + (-1, 32))
    amax = np.abs(blocks).max(-1, keepdims=True)
    byte = np.maximum(np.where(amax > 0, np.frexp(amax)[1] - 1 + 127, 0) - down, 1)
    scale = np.exp2(byte - 127.0)
    codes = (blocks / scale).astype(np.float32).astype(dtype).astype(np.float64)
    return np.moveaxis((codes * scale).reshape(v.shape), -1, axis)


WIDE = False


def mx_kscale(k):
    if not WIDE:
        return np.ones(k)
    levels = np.array([10, -10, 5, -5, 0])
    a = np.random.permutation(np.resize(levels, k // 512 * 4)).reshape(k // 512, 4)
    idx = np.arange(k)
    return np.exp2(a[idx // 512, idx % 128 // 32])


BF16 = ml_dtypes.bfloat16


def bf(x):
    return np.asarray(x, np.float32).astype(BF16)


def f64(x):
    return np.asarray(x).astype(np.float64)


B, S, E = 12, 512, 512


def setup_inputs():
    s = mx_kscale(E)
    q = np.random.standard_normal((B, S, E)) * 1.4 * s
    k = np.random.standard_normal((B, S, E)) * 1.4 / s
    v = np.random.standard_normal((B, S, E)) * 2.0
    return {"qkv": bf(np.concatenate([q, k, v], axis=-1))}


def reference(qkv):
    qkv = f64(qkv)
    E_ = qkv.shape[-1] // 3
    q = qkv[:, :, :E_]
    k = qkv[:, :, E_:2 * E_]
    v = qkv[:, :, 2 * E_:]
    q = q / np.sqrt(E_)
    scores = mxq(q, 2, "e4m3") @ mxq(k, 2, "e4m3").transpose(0, 2, 1)
    e = np.exp(scores - scores.max(-1, keepdims=True))
    probs = e / e.sum(-1, keepdims=True)
    return mxq(probs, 2, "e4m3") @ mxq(v, 1, "e4m3")

@@ -1,0 +1,236 @@
+import math
+from contextlib import ExitStack
+
+import concourse.mybir as mybir
+from concourse.masks import make_identity
+
+F32 = mybir.dt.float32
+BF16 = mybir.dt.bfloat16
+U32 = mybir.dt.uint32
+U8 = mybir.dt.uint8
+FP8X4 = mybir.dt.float8_e4m3fn_x4
+ALU = mybir.AluOpType
+ACT = mybir.ActivationFunctionType
+AX = mybir.AxisListType
+
+B, S, E = 12, 512, 512
+P = 128
+NT = B * 4
+FLOPS = 2 * 2 * B * S * S * E
+SCALE = 1.0 / math.sqrt(float(E))
+
+MANUAL = False
+
+
+def tile_scaleddotproductattention_t_kernel(tc, qkv, out):
+    nc = tc.nc
+    with ExitStack() as ctx:
+        const = ctx.enter_context(tc.tile_pool(name="const", bufs=1))
+        xpool = ctx.enter_context(tc.tile_pool(name="xpool", bufs=4))
+        prep = ctx.enter_context(tc.tile_pool(name="prep", bufs=2))
+        soft = ctx.enter_context(tc.tile_pool(name="soft", bufs=4))
+        pq = ctx.enter_context(tc.tile_pool(name="pq", bufs=3))
+        opool = ctx.enter_context(tc.tile_pool(name="opool", bufs=3))
+        psum = ctx.enter_context(tc.psum_pool(name="psum", bufs=2))
+
+        ident_f = const.tile([P, P], F32, name="ident_f")
+        make_identity(nc, ident_f[:])
+        ident_b = const.tile([P, P], BF16, name="ident_b")
+        make_identity(nc, ident_b[:])
+
+        x = {}
+        tpq = {}
+        tpk = {}
+        gqk = {}
+        cqk = {}
+        sqk = {}
+        gv = {}
+        cv = {}
+        sv = {}
+        sc = {}
+        nmx = {}
+        ex = {}
+        ssum = {}
+        pn = {}
+        pt = {}
+        gp = {}
+        cp = {}
+        sp = {}
+        ot = {}
+        o = {}
+
+        def load(b):
+            x[b] = xpool.tile([P, 4, 3 * E], BF16, name="x", tag="x")
+            nc.sync.dma_start(out=x[b][:], in_=qkv[b].rearrange("(p i) c -> p i c", i=4))
+
+        def tr_qk(b, h):
+            xf = x[b][:].rearrange("p i c -> p (i c)").bitcast(F32)
+            tpq[b, h] = psum.tile([P, 512], F32, name="tpq", tag="tp")
+            tpk[b, h] = psum.tile([P, 512], F32, name="tpk", tag="tp")
+            for which, dst in ((0, tpq[b, h]), (1, tpk[b, h])):
+                for u in range(2):
+                    for j in range(2):
+                        col = 768 * (2 * h + j) + 256 * which + 128 * u
+                        nc.tensor.transpose(
+                            dst[:, 256 * u + 128 * j : 256 * u + 128 * j + 128],
+                            xf[:, col : col + 128],
+                            ident_f[:],
+                        )
+
+        def cp_q(b, h):
+            if h == 0:
+                gqk[b] = prep.tile([P, 4096], BF16, name="gqk", tag="gqk", align_bytes=64)
+            nc.vector.tensor_scalar(
+                out=gqk[b][:, 1024 * h : 1024 * h + 1024].rearrange("p (n u e) -> p n u e", u=2, e=2),
+                in0=tpq[b, h][:].bitcast(BF16).rearrange("p (u n e) -> p n u e", u=2, e=2),
+                scalar1=SCALE,
+                scalar2=None,
+                op0=ALU.mult,
+            )
+
+        def cp_k(b, h):
+            gf = gqk[b][:].bitcast(F32)
+            nc.scalar.copy(
+                out=gf[:, 1024 + 512 * h : 1024 + 512 * h + 512].rearrange("p (n u) -> p n u", u=2),
+                in_=tpk[b, h][:].rearrange("p (u n) -> p n u", u=2),
+            )
+
+        def quant_qk(b):
+            cqk[b] = prep.tile([P, 1024], U32, name="cqk", tag="cqk", align_bytes=64)
+            sqk[b] = prep.tile([P, 1024], U8, name="sqk", tag="sqk", align_bytes=64)
+            nc.vector.quantize_mx(out=cqk[b][:].bitcast(FP8X4), scales=sqk[b][:], in_=gqk[b][:])
+
+        def regroup_v(b):
+            gv[b] = prep.tile([P, 2048], BF16, name="gv", tag="gv", align_bytes=64)
+            nc.vector.tensor_copy(
+                out=gv[b][:].rearrange("p (c i t) -> p c t i", i=4, t=4),
+                in_=x[b][:, :, 2 * E : 3 * E].rearrange("p t (c i) -> p c t i", i=4),
+            )
+
+        def quant_v(b):
+            cv[b] = prep.tile([P, 512], U32, name="cv", tag="cv", align_bytes=64, bufs=3)
+            sv[b] = prep.tile([P, 512], U8, name="sv", tag="sv", align_bytes=64, bufs=3)
+            nc.vector.quantize_mx(out=cv[b][:].bitcast(FP8X4), scales=sv[b][:], in_=gv[b][:])
+
+        def score(g):
+            b, i = divmod(g, 4)
+            sc[g] = psum.tile([P, 512], F32, name="sc", tag="sc")
+            nc.tensor.matmul_mx(
+                out=sc[g][:],
+                lhsT=cqk[b][:, 128 * i : 128 * i + 128].bitcast(FP8X4),
+                lhsT_scale=sqk[b][:, 128 * i : 128 * i + 128],
+                rhs=cqk[b][:, 512:1024].bitcast(FP8X4),
+                rhs_scale=sqk[b][:, 512:1024],
+                start=True,
+                stop=True,
+            )
+
+        def vmax(g):
+            nmx[g] = soft.tile([P, 1], F32, name="nmx", tag="nmx")
+            nc.vector.tensor_reduce(out=nmx[g][:], in_=sc[g][:], axis=AX.X, op=ALU.max, negate=True)
+
+        def vexp(g):
+            ex[g] = soft.tile([P, 512], F32, name="ex", tag="ex")
+            ssum[g] = soft.tile([P, 1], F32, name="ssum", tag="ssum")
+            nc.scalar.activation(
+                out=ex[g][:], in_=sc[g][:], func=ACT.Exp, bias=nmx[g][:, 0:1], scale=1.0, accum_out=ssum[g][:, 0:1]
+            )
+
+        def norm(g):
+            rs = soft.tile([P, 1], F32, name="rs", tag="rs")
+            nc.vector.reciprocal(out=rs[:], in_=ssum[g][:])
+            pn[g] = soft.tile([P, 512], BF16, name="pn", tag="pn")
+            nc.vector.tensor_scalar(out=pn[g][:], in0=ex[g][:], scalar1=rs[:, 0:1], scalar2=None, op0=ALU.mult)
+
+        def tr_p(g):
+            pair, j = divmod(g, 2)
+            if j == 0:
+                pt[pair] = psum.tile([P, 1024], BF16, name="pt", tag="pt")
+            for t in range(4):
+                nc.tensor.transpose(
+                    pt[pair][:, 256 * t + 128 * j : 256 * t + 128 * j + 128],
+                    pn[g][:, 128 * t : 128 * t + 128],
+                    ident_b[:],
+                )
+
+        def cp_p(pair):
+            gp[pair] = pq.tile([P, 1024], BF16, name="gp", tag="gp", align_bytes=64)
+            nc.scalar.copy(
+                out=gp[pair][:].rearrange("p (m t) -> p m t", t=4),
+                in_=pt[pair][:].rearrange("p (t m) -> p m t", t=4),
+            )
+
+        def quant_p(pair):
+            cp[pair] = pq.tile([P, 256], U32, name="cp", tag="cp", align_bytes=64)
+            sp[pair] = pq.tile([P, 256], U8, name="sp", tag="sp", align_bytes=64)
+            nc.vector.quantize_mx(out=cp[pair][:].bitcast(FP8X4), scales=sp[pair][:], in_=gp[pair][:])
+
+        def pv(g):
+            b = g // 4
+            pair, j = divmod(g, 2)
+            ot[g] = psum.tile([P, 512], F32, name="ot", tag="ot")
+            nc.tensor.matmul_mx(
+                out=ot[g][:],
+                lhsT=cp[pair][:, 128 * j : 128 * j + 128].bitcast(FP8X4),
+                lhsT_scale=sp[pair][:, 128 * j : 128 * j + 128],
+                rhs=cv[b][:].bitcast(FP8X4),
+                rhs_scale=sv[b][:],
+                start=True,
+                stop=True,
+            )
+
+        def cp_o(g):
+            b, i = divmod(g, 4)
+            if i == 0:
+                o[b] = opool.tile([P, 4, E], F32, name="o", tag="o")
+            nc.scalar.copy(out=o[b][:, i, :], in_=ot[g][:])
+
+        def store(b):
+            nc.sync.dma_start(out=out[b].rearrange("(p i) e -> p i e", i=4), in_=o[b][:])
+
+        def okb(b):
+            return 0 <= b < B
+
+        def okg(g):
+            return 0 <= g < NT
+
+        if MANUAL:
+            ctx.enter_context(tc.manual_schedule())
+
+        for b in range(4):
+            load(b)
+
+        for g in range(-8, NT + 8):
+            b, i = divmod(g, 4)
+            if i % 2 == 0:
+                if okg(g - 4):
+                    pv(g - 4)
+                    pv(g - 3)
+            if okg(g + 1):
+                score(g + 1)
+                vmax(g + 1)
+            if i % 2 == 1 and okb(b + 2):
+                tr_qk(b + 2, i // 2)
+            if okg(g):
+                vexp(g)
+                norm(g)
+                tr_p(g)
+            if okg(g - 4):
+                cp_o(g - 4)
+                if (g - 4) % 4 == 3:
+                    store((g - 4) // 4)
+            if i % 2 == 0 and okg(g - 2):
+                cp_p((g - 2) // 2)
+            if i % 2 == 1 and okg(g - 3):
+                quant_p((g - 3) // 2)
+            if i % 2 == 1 and okb(b + 2):
+                cp_q(b + 2, i // 2)
+                cp_k(b + 2, i // 2)
+            if i == 0 and okb(b + 1):
+                quant_qk(b + 1)
+            if i == 2 and okb(b + 1):
+                regroup_v(b + 1)
+                if okb(b + 5):
+                    load(b + 5)
+            if i == 3 and okb(b + 1):
+                quant_v(b + 1)

@@ -19,7 +19,9 @@ NT = B * 4
 FLOPS = 2 * 2 * B * S * S * E
 SCALE = 1.0 / math.sqrt(float(E))
 
-MANUAL = False
+POW_G = True
+LAST_V = 2
+TAIL_V = 8
 
 
 def tile_scaleddotproductattention_t_kernel(tc, qkv, out):
@@ -37,10 +39,11 @@ def tile_scaleddotproductattention_t_kernel(tc, qkv, out):
         make_identity(nc, ident_f[:])
         ident_b = const.tile([P, P], BF16, name="ident_b")
         make_identity(nc, ident_b[:])
+        neg1 = const.tile([P, 1], F32, name="neg1")
+        nc.vector.memset(neg1[:], -1.0)
 
         x = {}
-        tpq = {}
-        tpk = {}
+        tp = {}
         gqk = {}
         cqk = {}
         sqk = {}
@@ -59,30 +62,31 @@ def tile_scaleddotproductattention_t_kernel(tc, qkv, out):
         ot = {}
         o = {}
 
-        def load(b):
+        def new_x(b):
             x[b] = xpool.tile([P, 4, 3 * E], BF16, name="x", tag="x")
-            nc.sync.dma_start(out=x[b][:], in_=qkv[b].rearrange("(p i) c -> p i c", i=4))
 
-        def tr_qk(b, h):
+        def load(b, i0, i1, c0, c1):
+            src = qkv[b].rearrange("(p i) c -> p i c", i=4)
+            nc.sync.dma_start(out=x[b][:, i0:i1, c0:c1], in_=src[:, i0:i1, c0:c1])
+
+        def trx(b, h, w):
             xf = x[b][:].rearrange("p i c -> p (i c)").bitcast(F32)
-            tpq[b, h] = psum.tile([P, 512], F32, name="tpq", tag="tp")
-            tpk[b, h] = psum.tile([P, 512], F32, name="tpk", tag="tp")
-            for which, dst in ((0, tpq[b, h]), (1, tpk[b, h])):
-                for u in range(2):
-                    for j in range(2):
-                        col = 768 * (2 * h + j) + 256 * which + 128 * u
-                        nc.tensor.transpose(
-                            dst[:, 256 * u + 128 * j : 256 * u + 128 * j + 128],
-                            xf[:, col : col + 128],
-                            ident_f[:],
-                        )
+            tp[b, h, w] = psum.tile([P, 512], F32, name="tp", tag="tp")
+            for u in range(2):
+                for j in range(2):
+                    col = 768 * (2 * h + j) + 256 * w + 128 * u
+                    nc.tensor.transpose(
+                        tp[b, h, w][:, 256 * u + 128 * j : 256 * u + 128 * j + 128],
+                        xf[:, col : col + 128],
+                        ident_f[:],
+                    )
 
         def cp_q(b, h):
             if h == 0:
                 gqk[b] = prep.tile([P, 4096], BF16, name="gqk", tag="gqk", align_bytes=64)
             nc.vector.tensor_scalar(
                 out=gqk[b][:, 1024 * h : 1024 * h + 1024].rearrange("p (n u e) -> p n u e", u=2, e=2),
-                in0=tpq[b, h][:].bitcast(BF16).rearrange("p (u n e) -> p n u e", u=2, e=2),
+                in0=tp[b, h, 0][:].bitcast(BF16).rearrange("p (u n e) -> p n u e", u=2, e=2),
                 scalar1=SCALE,
                 scalar2=None,
                 op0=ALU.mult,
@@ -92,7 +96,7 @@ def tile_scaleddotproductattention_t_kernel(tc, qkv, out):
             gf = gqk[b][:].bitcast(F32)
             nc.scalar.copy(
                 out=gf[:, 1024 + 512 * h : 1024 + 512 * h + 512].rearrange("p (n u) -> p n u", u=2),
-                in_=tpk[b, h][:].rearrange("p (u n) -> p n u", u=2),
+                in_=tp[b, h, 1][:].rearrange("p (u n) -> p n u", u=2),
             )
 
         def quant_qk(b):
@@ -108,8 +112,8 @@ def tile_scaleddotproductattention_t_kernel(tc, qkv, out):
             )
 
         def quant_v(b):
-            cv[b] = prep.tile([P, 512], U32, name="cv", tag="cv", align_bytes=64, bufs=3)
-            sv[b] = prep.tile([P, 512], U8, name="sv", tag="sv", align_bytes=64, bufs=3)
+            cv[b] = prep.tile([P, 512], U32, name="cv", tag="cv", align_bytes=64)
+            sv[b] = prep.tile([P, 512], U8, name="sv", tag="sv", align_bytes=64)
             nc.vector.quantize_mx(out=cv[b][:].bitcast(FP8X4), scales=sv[b][:], in_=gv[b][:])
 
         def score(g):
@@ -137,10 +141,19 @@ def tile_scaleddotproductattention_t_kernel(tc, qkv, out):
             )
 
         def norm(g):
+            on_g = g < NT - LAST_V
             rs = soft.tile([P, 1], F32, name="rs", tag="rs")
-            nc.vector.reciprocal(out=rs[:], in_=ssum[g][:])
             pn[g] = soft.tile([P, 512], BF16, name="pn", tag="pn")
-            nc.vector.tensor_scalar(out=pn[g][:], in0=ex[g][:], scalar1=rs[:, 0:1], scalar2=None, op0=ALU.mult)
+            if on_g and POW_G:
+                nc.gpsimd.tensor_tensor(out=rs[:], in0=ssum[g][:], in1=neg1[:], op=ALU.pow)
+            else:
+                nc.vector.reciprocal(out=rs[:], in_=ssum[g][:])
+            if on_g:
+                nc.gpsimd.tensor_scalar(
+                    out=pn[g][:], in0=ex[g][:], scalar1=rs[:, 0:1], scalar2=0.0, op0=ALU.mult, op1=ALU.add
+                )
+            else:
+                nc.vector.tensor_scalar(out=pn[g][:], in0=ex[g][:], scalar1=rs[:, 0:1], scalar2=None, op0=ALU.mult)
 
         def tr_p(g):
             pair, j = divmod(g, 2)
@@ -179,14 +192,19 @@ def tile_scaleddotproductattention_t_kernel(tc, qkv, out):
                 stop=True,
             )
 
-        def cp_o(g):
+        def cp_o(g, on_vector):
             b, i = divmod(g, 4)
             if i == 0:
                 o[b] = opool.tile([P, 4, E], F32, name="o", tag="o")
-            nc.scalar.copy(out=o[b][:, i, :], in_=ot[g][:])
-
-        def store(b):
-            nc.sync.dma_start(out=out[b].rearrange("(p i) e -> p i e", i=4), in_=o[b][:])
+            if on_vector:
+                nc.vector.tensor_copy(out=o[b][:, i, :], in_=ot[g][:])
+            else:
+                nc.scalar.copy(out=o[b][:, i, :], in_=ot[g][:])
+            dst = out[b].rearrange("(p i) e -> p i e", i=4)
+            if b == B - 1:
+                nc.sync.dma_start(out=dst[:, i, :], in_=o[b][:, i, :])
+            elif i % 2 == 1:
+                nc.sync.dma_start(out=dst[:, i - 1 : i + 1, :], in_=o[b][:, i - 1 : i + 1, :])
 
         def okb(b):
             return 0 <= b < B
@@ -194,43 +212,58 @@ def tile_scaleddotproductattention_t_kernel(tc, qkv, out):
         def okg(g):
             return 0 <= g < NT
 
-        if MANUAL:
-            ctx.enter_context(tc.manual_schedule())
+        ctx.enter_context(tc.manual_schedule())
 
         for b in range(4):
-            load(b)
+            new_x(b)
+        load(0, 0, 2, 0, 2 * E)
+        load(0, 2, 4, 0, 2 * E)
+        load(1, 0, 4, 0, 2 * E)
+        load(0, 0, 4, 2 * E, 3 * E)
+        load(1, 0, 4, 2 * E, 3 * E)
+        load(2, 0, 4, 0, 3 * E)
+        load(3, 0, 4, 0, 3 * E)
 
-        for g in range(-8, NT + 8):
+        for g in range(-8, NT + 6):
             b, i = divmod(g, 4)
-            if i % 2 == 0:
-                if okg(g - 4):
-                    pv(g - 4)
-                    pv(g - 3)
+            t5 = g - 5
+            o_on_v = i == 3 or (t5 >= NT - TAIL_V and i % 2 == 1)
             if okg(g + 1):
-                score(g + 1)
                 vmax(g + 1)
-            if i % 2 == 1 and okb(b + 2):
-                tr_qk(b + 2, i // 2)
+            if i % 2 == 0 and okg(g - 4):
+                quant_p((g - 4) // 2)
+            if i == 1 and okb(b + 1):
+                quant_qk(b + 1)
+            if i == 0 and okb(b):
+                regroup_v(b)
+                if okb(b + 4):
+                    new_x(b + 4)
+                    load(b + 4, 0, 4, 0, 3 * E)
+            if i == 2 and okb(b):
+                quant_v(b)
             if okg(g):
                 vexp(g)
-                norm(g)
-                tr_p(g)
+            if okg(g + 2):
+                score(g + 2)
             if okg(g - 4):
-                cp_o(g - 4)
-                if (g - 4) % 4 == 3:
-                    store((g - 4) // 4)
-            if i % 2 == 0 and okg(g - 2):
-                cp_p((g - 2) // 2)
+                pv(g - 4)
+            if okg(g - 1):
+                tr_p(g - 1)
+            if okb(b + 2):
+                trx(b + 2, i // 2, i % 2)
             if i % 2 == 1 and okg(g - 3):
-                quant_p((g - 3) // 2)
-            if i % 2 == 1 and okb(b + 2):
-                cp_q(b + 2, i // 2)
-                cp_k(b + 2, i // 2)
+                cp_p((g - 3) // 2)
+            if okg(t5) and not o_on_v:
+                cp_o(t5, False)
+            if i == 2 and okb(b + 2):
+                cp_k(b + 2, 0)
             if i == 0 and okb(b + 1):
-                quant_qk(b + 1)
-            if i == 2 and okb(b + 1):
-                regroup_v(b + 1)
-                if okb(b + 5):
-                    load(b + 5)
-            if i == 3 and okb(b + 1):
-                quant_v(b + 1)
+                cp_k(b + 1, 1)
+            if i == 1 and okb(b + 2):
+                cp_q(b + 2, 0)
+            if i == 3 and okb(b + 2):
+                cp_q(b + 2, 1)
+            if okg(t5) and o_on_v:
+                cp_o(t5, True)
+            if okg(g):
+                norm(g)

@@ -22,6 +22,7 @@ SCALE = 1.0 / math.sqrt(float(E))
 POW_G = True
 LAST_V = 2
 TAIL_V = 8
+DUP_PV = 2
 
 
 def tile_scaleddotproductattention_t_kernel(tc, qkv, out):
@@ -182,15 +183,16 @@ def tile_scaleddotproductattention_t_kernel(tc, qkv, out):
             b = g // 4
             pair, j = divmod(g, 2)
             ot[g] = psum.tile([P, 512], F32, name="ot", tag="ot")
-            nc.tensor.matmul_mx(
-                out=ot[g][:],
-                lhsT=cp[pair][:, 128 * j : 128 * j + 128].bitcast(FP8X4),
-                lhsT_scale=sp[pair][:, 128 * j : 128 * j + 128],
-                rhs=cv[b][:].bitcast(FP8X4),
-                rhs_scale=sv[b][:],
-                start=True,
-                stop=True,
-            )
+            for rep in range(DUP_PV):
+                nc.tensor.matmul_mx(
+                    out=ot[g][:],
+                    lhsT=cp[pair][:, 128 * j : 128 * j + 128].bitcast(FP8X4),
+                    lhsT_scale=sp[pair][:, 128 * j : 128 * j + 128],
+                    rhs=cv[b][:].bitcast(FP8X4),
+                    rhs_scale=sv[b][:],
+                    start=True,
+                    stop=True,
+                )
 
         def cp_o(g, on_vector):
             b, i = divmod(g, 4)

@@ -20,9 +20,9 @@ FLOPS = 2 * 2 * B * S * S * E
 SCALE = 1.0 / math.sqrt(float(E))
 
 POW_G = True
-LAST_V = 2
+USE_G = False
+LAST_V = 2 if USE_G else NT
 TAIL_V = 8
-DUP_PV = 2
 
 
 def tile_scaleddotproductattention_t_kernel(tc, qkv, out):
@@ -183,16 +183,15 @@ def tile_scaleddotproductattention_t_kernel(tc, qkv, out):
             b = g // 4
             pair, j = divmod(g, 2)
             ot[g] = psum.tile([P, 512], F32, name="ot", tag="ot")
-            for rep in range(DUP_PV):
-                nc.tensor.matmul_mx(
-                    out=ot[g][:],
-                    lhsT=cp[pair][:, 128 * j : 128 * j + 128].bitcast(FP8X4),
-                    lhsT_scale=sp[pair][:, 128 * j : 128 * j + 128],
-                    rhs=cv[b][:].bitcast(FP8X4),
-                    rhs_scale=sv[b][:],
-                    start=True,
-                    stop=True,
-                )
+            nc.tensor.matmul_mx(
+                out=ot[g][:],
+                lhsT=cp[pair][:, 128 * j : 128 * j + 128].bitcast(FP8X4),
+                lhsT_scale=sp[pair][:, 128 * j : 128 * j + 128],
+                rhs=cv[b][:].bitcast(FP8X4),
+                rhs_scale=sv[b][:],
+                start=True,
+                stop=True,
+            )
 
         def cp_o(g, on_vector):
             b, i = divmod(g, 4)
@@ -226,10 +225,10 @@ def tile_scaleddotproductattention_t_kernel(tc, qkv, out):
         load(2, 0, 4, 0, 3 * E)
         load(3, 0, 4, 0, 3 * E)
 
-        for g in range(-8, NT + 6):
+        for g in range(-8, NT + 7):
             b, i = divmod(g, 4)
-            t5 = g - 5
-            o_on_v = i == 3 or (t5 >= NT - TAIL_V and i % 2 == 1)
+            t5 = g - 6
+            o_on_v = (USE_G and i == 3) or (t5 >= NT - TAIL_V and i % 2 == 1)
             if okg(g + 1):
                 vmax(g + 1)
             if i % 2 == 0 and okg(g - 4):
@@ -245,10 +244,10 @@ def tile_scaleddotproductattention_t_kernel(tc, qkv, out):
                 quant_v(b)
             if okg(g):
                 vexp(g)
+            if okg(g - 5):
+                pv(g - 5)
             if okg(g + 2):
                 score(g + 2)
-            if okg(g - 4):
-                pv(g - 4)
             if okg(g - 1):
                 tr_p(g - 1)
             if okb(b + 2):

@@ -19,9 +19,7 @@ NT = B * 4
 FLOPS = 2 * 2 * B * S * S * E
 SCALE = 1.0 / math.sqrt(float(E))
 
-POW_G = True
-USE_G = False
-LAST_V = 2 if USE_G else NT
+G_TT = True
 TAIL_V = 8
 
 
@@ -34,7 +32,7 @@ def tile_scaleddotproductattention_t_kernel(tc, qkv, out):
         soft = ctx.enter_context(tc.tile_pool(name="soft", bufs=4))
         pq = ctx.enter_context(tc.tile_pool(name="pq", bufs=3))
         opool = ctx.enter_context(tc.tile_pool(name="opool", bufs=3))
-        psum = ctx.enter_context(tc.psum_pool(name="psum", bufs=2))
+        psum = ctx.enter_context(tc.psum_pool(name="psum", bufs=1))
 
         ident_f = const.tile([P, P], F32, name="ident_f")
         make_identity(nc, ident_f[:])
@@ -55,6 +53,7 @@ def tile_scaleddotproductattention_t_kernel(tc, qkv, out):
         nmx = {}
         ex = {}
         ssum = {}
+        rs = {}
         pn = {}
         pt = {}
         gp = {}
@@ -72,7 +71,7 @@ def tile_scaleddotproductattention_t_kernel(tc, qkv, out):
 
         def trx(b, h, w):
             xf = x[b][:].rearrange("p i c -> p (i c)").bitcast(F32)
-            tp[b, h, w] = psum.tile([P, 512], F32, name="tp", tag="tp")
+            tp[b, h, w] = psum.tile([P, 512], F32, name="tp", tag="tp%d" % w)
             for u in range(2):
                 for j in range(2):
                     col = 768 * (2 * h + j) + 256 * w + 128 * u
@@ -119,7 +118,7 @@ def tile_scaleddotproductattention_t_kernel(tc, qkv, out):
 
         def score(g):
             b, i = divmod(g, 4)
-            sc[g] = psum.tile([P, 512], F32, name="sc", tag="sc")
+            sc[g] = psum.tile([P, 512], F32, name="sc", tag="sc%d" % (g % 2))
             nc.tensor.matmul_mx(
                 out=sc[g][:],
                 lhsT=cqk[b][:, 128 * i : 128 * i + 128].bitcast(FP8X4),
@@ -141,25 +140,32 @@ def tile_scaleddotproductattention_t_kernel(tc, qkv, out):
                 out=ex[g][:], in_=sc[g][:], func=ACT.Exp, bias=nmx[g][:, 0:1], scale=1.0, accum_out=ssum[g][:, 0:1]
             )
 
-        def norm(g):
-            on_g = g < NT - LAST_V
-            rs = soft.tile([P, 1], F32, name="rs", tag="rs")
-            pn[g] = soft.tile([P, 512], BF16, name="pn", tag="pn")
-            if on_g and POW_G:
-                nc.gpsimd.tensor_tensor(out=rs[:], in0=ssum[g][:], in1=neg1[:], op=ALU.pow)
-            else:
-                nc.vector.reciprocal(out=rs[:], in_=ssum[g][:])
+        def recip(g, on_g):
+            rs[g] = soft.tile([P, 1], F32, name="rs", tag="rs")
             if on_g:
+                nc.gpsimd.tensor_tensor(out=rs[g][:], in0=ssum[g][:], in1=neg1[:], op=ALU.pow)
+            else:
+                nc.vector.reciprocal(out=rs[g][:], in_=ssum[g][:])
+
+        def norm(g, on_g):
+            pn[g] = soft.tile([P, 512], BF16, name="pn", tag="pn")
+            if on_g and G_TT:
+                nc.gpsimd.tensor_tensor(
+                    out=pn[g][:], in0=ex[g][:], in1=rs[g][:, 0:1].to_broadcast([P, 512]), op=ALU.mult
+                )
+            elif on_g:
                 nc.gpsimd.tensor_scalar(
-                    out=pn[g][:], in0=ex[g][:], scalar1=rs[:, 0:1], scalar2=0.0, op0=ALU.mult, op1=ALU.add
+                    out=pn[g][:], in0=ex[g][:], scalar1=rs[g][:, 0:1], scalar2=0.0, op0=ALU.mult, op1=ALU.add
                 )
             else:
-                nc.vector.tensor_scalar(out=pn[g][:], in0=ex[g][:], scalar1=rs[:, 0:1], scalar2=None, op0=ALU.mult)
+                nc.vector.tensor_scalar(
+                    out=pn[g][:], in0=ex[g][:], scalar1=rs[g][:, 0:1], scalar2=None, op0=ALU.mult
+                )
 
         def tr_p(g):
             pair, j = divmod(g, 2)
             if j == 0:
-                pt[pair] = psum.tile([P, 1024], BF16, name="pt", tag="pt")
+                pt[pair] = psum.tile([P, 1024], BF16, name="pt", tag="pt%d" % (pair % 2))
             for t in range(4):
                 nc.tensor.transpose(
                     pt[pair][:, 256 * t + 128 * j : 256 * t + 128 * j + 128],
@@ -182,7 +188,7 @@ def tile_scaleddotproductattention_t_kernel(tc, qkv, out):
         def pv(g):
             b = g // 4
             pair, j = divmod(g, 2)
-            ot[g] = psum.tile([P, 512], F32, name="ot", tag="ot")
+            ot[g] = psum.tile([P, 512], F32, name="ot", tag="ot%d" % (g % 2))
             nc.tensor.matmul_mx(
                 out=ot[g][:],
                 lhsT=cp[pair][:, 128 * j : 128 * j + 128].bitcast(FP8X4),
@@ -228,9 +234,15 @@ def tile_scaleddotproductattention_t_kernel(tc, qkv, out):
         for g in range(-8, NT + 7):
             b, i = divmod(g, 4)
             t5 = g - 6
-            o_on_v = (USE_G and i == 3) or (t5 >= NT - TAIL_V and i % 2 == 1)
+            o_on_v = t5 >= NT - TAIL_V and i % 2 == 1
             if okg(g + 1):
                 vmax(g + 1)
+            if i % 2 == 0 and okg(g - 1) and g - 1 < NT - 2:
+                norm(g - 1, False)
+            if i == 1 and okb(b + 2):
+                cp_q(b + 2, 0)
+            if i == 3 and okb(b + 2):
+                cp_q(b + 2, 1)
             if i % 2 == 0 and okg(g - 4):
                 quant_p((g - 4) // 2)
             if i == 1 and okb(b + 1):
@@ -260,11 +272,14 @@ def tile_scaleddotproductattention_t_kernel(tc, qkv, out):
                 cp_k(b + 2, 0)
             if i == 0 and okb(b + 1):
                 cp_k(b + 1, 1)
-            if i == 1 and okb(b + 2):
-                cp_q(b + 2, 0)
-            if i == 3 and okb(b + 2):
-                cp_q(b + 2, 1)
             if okg(t5) and o_on_v:
                 cp_o(t5, True)
             if okg(g):
-                norm(g)
+                if g >= NT - 2:
+                    recip(g, False)
+                    norm(g, False)
+                elif i % 2 == 0:
+                    recip(g, False)
+                    norm(g, True)
+                else:
+                    recip(g, True)

@@ -20,6 +20,7 @@ FLOPS = 2 * 2 * B * S * S * E
 SCALE = 1.0 / math.sqrt(float(E))
 
 G_TT = True
+NORM_ENG = "VVVS"
 TAIL_V = 8
 
 
@@ -147,9 +148,11 @@ def tile_scaleddotproductattention_t_kernel(tc, qkv, out):
             else:
                 nc.vector.reciprocal(out=rs[g][:], in_=ssum[g][:])
 
-        def norm(g, on_g):
+        def norm(g, on_g, on_s=False):
             pn[g] = soft.tile([P, 512], BF16, name="pn", tag="pn")
-            if on_g and G_TT:
+            if on_s:
+                nc.scalar.activation(out=pn[g][:], in_=ex[g][:], func=ACT.Copy, scale=rs[g][:, 0:1])
+            elif on_g and G_TT:
                 nc.gpsimd.tensor_tensor(
                     out=pn[g][:], in0=ex[g][:], in1=rs[g][:, 0:1].to_broadcast([P, 512]), op=ALU.mult
                 )
@@ -237,7 +240,7 @@ def tile_scaleddotproductattention_t_kernel(tc, qkv, out):
             o_on_v = t5 >= NT - TAIL_V and i % 2 == 1
             if okg(g + 1):
                 vmax(g + 1)
-            if i % 2 == 0 and okg(g - 1) and g - 1 < NT - 2:
+            if okg(g - 1) and g - 1 < NT - 2 and (NORM_ENG[(g - 1) % 4] == "V" or g - 1 >= NT - 8):
                 norm(g - 1, False)
             if i == 1 and okb(b + 2):
                 cp_q(b + 2, 0)
@@ -256,6 +259,8 @@ def tile_scaleddotproductattention_t_kernel(tc, qkv, out):
                 quant_v(b)
             if okg(g):
                 vexp(g)
+            if okg(g - 1) and g - 1 < NT - 8 and NORM_ENG[(g - 1) % 4] == "S":
+                norm(g - 1, False, True)
             if okg(g - 5):
                 pv(g - 5)
             if okg(g + 2):
@@ -278,7 +283,7 @@ def tile_scaleddotproductattention_t_kernel(tc, qkv, out):
                 if g >= NT - 2:
                     recip(g, False)
                     norm(g, False)
-                elif i % 2 == 0:
+                elif NORM_ENG[i] == "G":
                     recip(g, False)
                     norm(g, True)
                 else:

@@ -43,6 +43,7 @@ def tile_scaleddotproductattention_t_kernel(tc, qkv, out):
         nc.vector.memset(neg1[:], -1.0)
 
         x = {}
+        xv = {}
         tp = {}
         gqk = {}
         cqk = {}
@@ -63,19 +64,24 @@ def tile_scaleddotproductattention_t_kernel(tc, qkv, out):
         ot = {}
         o = {}
 
-        def new_x(b):
-            x[b] = xpool.tile([P, 4, 3 * E], BF16, name="x", tag="x")
-
-        def load(b, i0, i1, c0, c1):
+        def load_qk(b, parts):
+            x[b] = xpool.tile([P, 4, 2 * E], BF16, name="xqk", tag="xqk", bufs=3)
             src = qkv[b].rearrange("(p i) c -> p i c", i=4)
-            nc.sync.dma_start(out=x[b][:, i0:i1, c0:c1], in_=src[:, i0:i1, c0:c1])
+            step = 4 // parts
+            for i0 in range(0, 4, step):
+                nc.sync.dma_start(out=x[b][:, i0 : i0 + step, :], in_=src[:, i0 : i0 + step, 0 : 2 * E])
+
+        def load_v(b):
+            xv[b] = xpool.tile([P, 4, E], BF16, name="xv", tag="xv", bufs=4)
+            src = qkv[b].rearrange("(p i) c -> p i c", i=4)
+            nc.sync.dma_start(out=xv[b][:], in_=src[:, :, 2 * E : 3 * E])
 
         def trx(b, h, w):
             xf = x[b][:].rearrange("p i c -> p (i c)").bitcast(F32)
             tp[b, h, w] = psum.tile([P, 512], F32, name="tp", tag="tp%d" % w)
             for u in range(2):
                 for j in range(2):
-                    col = 768 * (2 * h + j) + 256 * w + 128 * u
+                    col = 512 * (2 * h + j) + 256 * w + 128 * u
                     nc.tensor.transpose(
                         tp[b, h, w][:, 256 * u + 128 * j : 256 * u + 128 * j + 128],
                         xf[:, col : col + 128],
@@ -85,13 +91,12 @@ def tile_scaleddotproductattention_t_kernel(tc, qkv, out):
         def cp_q(b, h):
             if h == 0:
                 gqk[b] = prep.tile([P, 4096], BF16, name="gqk", tag="gqk", align_bytes=64)
-            nc.vector.tensor_scalar(
-                out=gqk[b][:, 1024 * h : 1024 * h + 1024].rearrange("p (n u e) -> p n u e", u=2, e=2),
-                in0=tp[b, h, 0][:].bitcast(BF16).rearrange("p (u n e) -> p n u e", u=2, e=2),
-                scalar1=SCALE,
-                scalar2=None,
-                op0=ALU.mult,
-            )
+            dst = gqk[b][:, 1024 * h : 1024 * h + 1024].rearrange("p (n u e) -> p n u e", u=2, e=2)
+            src = tp[b, h, 0][:].bitcast(BF16).rearrange("p (u n e) -> p n u e", u=2, e=2)
+            if b == 1:
+                nc.scalar.activation(out=dst, in_=src, func=ACT.Copy, scale=SCALE)
+            else:
+                nc.vector.tensor_scalar(out=dst, in0=src, scalar1=SCALE, scalar2=None, op0=ALU.mult)
 
         def cp_k(b, h):
             gf = gqk[b][:].bitcast(F32)
@@ -109,7 +114,7 @@ def tile_scaleddotproductattention_t_kernel(tc, qkv, out):
             gv[b] = prep.tile([P, 2048], BF16, name="gv", tag="gv", align_bytes=64)
             nc.vector.tensor_copy(
                 out=gv[b][:].rearrange("p (c i t) -> p c t i", i=4, t=4),
-                in_=x[b][:, :, 2 * E : 3 * E].rearrange("p t (c i) -> p c t i", i=4),
+                in_=xv[b][:].rearrange("p t (c i) -> p c t i", i=4),
             )
 
         def quant_v(b):
@@ -224,15 +229,13 @@ def tile_scaleddotproductattention_t_kernel(tc, qkv, out):
 
         ctx.enter_context(tc.manual_schedule())
 
-        for b in range(4):
-            new_x(b)
-        load(0, 0, 2, 0, 2 * E)
-        load(0, 2, 4, 0, 2 * E)
-        load(1, 0, 4, 0, 2 * E)
-        load(0, 0, 4, 2 * E, 3 * E)
-        load(1, 0, 4, 2 * E, 3 * E)
-        load(2, 0, 4, 0, 3 * E)
-        load(3, 0, 4, 0, 3 * E)
+        load_qk(0, 2)
+        load_qk(1, 1)
+        load_v(0)
+        load_qk(2, 1)
+        load_v(1)
+        load_v(2)
+        load_v(3)
 
         for g in range(-8, NT + 7):
             b, i = divmod(g, 4)
@@ -253,8 +256,7 @@ def tile_scaleddotproductattention_t_kernel(tc, qkv, out):
             if i == 0 and okb(b):
                 regroup_v(b)
                 if okb(b + 4):
-                    new_x(b + 4)
-                    load(b + 4, 0, 4, 0, 3 * E)
+                    load_v(b + 4)
             if i == 2 and okb(b):
                 quant_v(b)
             if okg(g):
@@ -269,6 +271,8 @@ def tile_scaleddotproductattention_t_kernel(tc, qkv, out):
                 tr_p(g - 1)
             if okb(b + 2):
                 trx(b + 2, i // 2, i % 2)
+                if i == 3 and okb(b + 5):
+                    load_qk(b + 5, 1)
             if i % 2 == 1 and okg(g - 3):
                 cp_p((g - 3) // 2)
             if okg(t5) and not o_on_v:

import math
from contextlib import ExitStack

import concourse.mybir as mybir
from concourse.masks import make_identity

F32 = mybir.dt.float32
BF16 = mybir.dt.bfloat16
U32 = mybir.dt.uint32
U8 = mybir.dt.uint8
FP8X4 = mybir.dt.float8_e4m3fn_x4
ALU = mybir.AluOpType
ACT = mybir.ActivationFunctionType
AX = mybir.AxisListType

B, S, E = 12, 512, 512
P = 128
NT = B * 4
FLOPS = 2 * 2 * B * S * S * E
SCALE = 1.0 / math.sqrt(float(E))

G_TT = True
NORM_ENG = "VVVS"
TAIL_V = 8


def tile_scaleddotproductattention_t_kernel(tc, qkv, out):
    nc = tc.nc
    with ExitStack() as ctx:
        const = ctx.enter_context(tc.tile_pool(name="const", bufs=1))
        xpool = ctx.enter_context(tc.tile_pool(name="xpool", bufs=4))
        prep = ctx.enter_context(tc.tile_pool(name="prep", bufs=2))
        soft = ctx.enter_context(tc.tile_pool(name="soft", bufs=4))
        pq = ctx.enter_context(tc.tile_pool(name="pq", bufs=3))
        opool = ctx.enter_context(tc.tile_pool(name="opool", bufs=3))
        psum = ctx.enter_context(tc.psum_pool(name="psum", bufs=1))

        ident_f = const.tile([P, P], F32, name="ident_f")
        make_identity(nc, ident_f[:])
        ident_b = const.tile([P, P], BF16, name="ident_b")
        make_identity(nc, ident_b[:])
        neg1 = const.tile([P, 1], F32, name="neg1")
        nc.vector.memset(neg1[:], -1.0)

        x = {}
        xv = {}
        tp = {}
        gqk = {}
        cqk = {}
        sqk = {}
        gv = {}
        cv = {}
        sv = {}
        sc = {}
        nmx = {}
        ex = {}
        ssum = {}
        rs = {}
        pn = {}
        pt = {}
        gp = {}
        cp = {}
        sp = {}
        ot = {}
        o = {}

        def load_qk(b, parts):
            x[b] = xpool.tile([P, 4, 2 * E], BF16, name="xqk", tag="xqk", bufs=3)
            src = qkv[b].rearrange("(p i) c -> p i c", i=4)
            step = 4 // parts
            for i0 in range(0, 4, step):
                nc.sync.dma_start(out=x[b][:, i0 : i0 + step, :], in_=src[:, i0 : i0 + step, 0 : 2 * E])

        def load_v(b):
            xv[b] = xpool.tile([P, 4, E], BF16, name="xv", tag="xv", bufs=4)
            src = qkv[b].rearrange("(p i) c -> p i c", i=4)
            nc.sync.dma_start(out=xv[b][:], in_=src[:, :, 2 * E : 3 * E])

        def trx(b, h, w):
            xf = x[b][:].rearrange("p i c -> p (i c)").bitcast(F32)
            tp[b, h, w] = psum.tile([P, 512], F32, name="tp", tag="tp%d" % w)
            for u in range(2):
                for j in range(2):
                    col = 512 * (2 * h + j) + 256 * w + 128 * u
                    nc.tensor.transpose(
                        tp[b, h, w][:, 256 * u + 128 * j : 256 * u + 128 * j + 128],
                        xf[:, col : col + 128],
                        ident_f[:],
                    )

        def cp_q(b, h):
            if h == 0:
                gqk[b] = prep.tile([P, 4096], BF16, name="gqk", tag="gqk", align_bytes=64)
            dst = gqk[b][:, 1024 * h : 1024 * h + 1024].rearrange("p (n u e) -> p n u e", u=2, e=2)
            src = tp[b, h, 0][:].bitcast(BF16).rearrange("p (u n e) -> p n u e", u=2, e=2)
            if b == 1:
                nc.scalar.activation(out=dst, in_=src, func=ACT.Copy, scale=SCALE)
            else:
                nc.vector.tensor_scalar(out=dst, in0=src, scalar1=SCALE, scalar2=None, op0=ALU.mult)

        def cp_k(b, h):
            gf = gqk[b][:].bitcast(F32)
            nc.scalar.copy(
                out=gf[:, 1024 + 512 * h : 1024 + 512 * h + 512].rearrange("p (n u) -> p n u", u=2),
                in_=tp[b, h, 1][:].rearrange("p (u n) -> p n u", u=2),
            )

        def quant_qk(b):
            cqk[b] = prep.tile([P, 1024], U32, name="cqk", tag="cqk", align_bytes=64)
            sqk[b] = prep.tile([P, 1024], U8, name="sqk", tag="sqk", align_bytes=64)
            nc.vector.quantize_mx(out=cqk[b][:].bitcast(FP8X4), scales=sqk[b][:], in_=gqk[b][:])

        def regroup_v(b):
            gv[b] = prep.tile([P, 2048], BF16, name="gv", tag="gv", align_bytes=64)
            nc.vector.tensor_copy(
                out=gv[b][:].rearrange("p (c i t) -> p c t i", i=4, t=4),
                in_=xv[b][:].rearrange("p t (c i) -> p c t i", i=4),
            )

        def quant_v(b):
            cv[b] = prep.tile([P, 512], U32, name="cv", tag="cv", align_bytes=64)
            sv[b] = prep.tile([P, 512], U8, name="sv", tag="sv", align_bytes=64)
            nc.vector.quantize_mx(out=cv[b][:].bitcast(FP8X4), scales=sv[b][:], in_=gv[b][:])

        def score(g):
            b, i = divmod(g, 4)
            sc[g] = psum.tile([P, 512], F32, name="sc", tag="sc%d" % (g % 2))
            nc.tensor.matmul_mx(
                out=sc[g][:],
                lhsT=cqk[b][:, 128 * i : 128 * i + 128].bitcast(FP8X4),
                lhsT_scale=sqk[b][:, 128 * i : 128 * i + 128],
                rhs=cqk[b][:, 512:1024].bitcast(FP8X4),
                rhs_scale=sqk[b][:, 512:1024],
                start=True,
                stop=True,
            )

        def vmax(g):
            nmx[g] = soft.tile([P, 1], F32, name="nmx", tag="nmx")
            nc.vector.tensor_reduce(out=nmx[g][:], in_=sc[g][:], axis=AX.X, op=ALU.max, negate=True)

        def vexp(g):
            ex[g] = soft.tile([P, 512], F32, name="ex", tag="ex")
            ssum[g] = soft.tile([P, 1], F32, name="ssum", tag="ssum")
            nc.scalar.activation(
                out=ex[g][:], in_=sc[g][:], func=ACT.Exp, bias=nmx[g][:, 0:1], scale=1.0, accum_out=ssum[g][:, 0:1]
            )

        def recip(g, on_g):
            rs[g] = soft.tile([P, 1], F32, name="rs", tag="rs")
            if on_g:
                nc.gpsimd.tensor_tensor(out=rs[g][:], in0=ssum[g][:], in1=neg1[:], op=ALU.pow)
            else:
                nc.vector.reciprocal(out=rs[g][:], in_=ssum[g][:])

        def norm(g, on_g, on_s=False):
            pn[g] = soft.tile([P, 512], BF16, name="pn", tag="pn")
            if on_s:
                nc.scalar.activation(out=pn[g][:], in_=ex[g][:], func=ACT.Copy, scale=rs[g][:, 0:1])
            elif on_g and G_TT:
                nc.gpsimd.tensor_tensor(
                    out=pn[g][:], in0=ex[g][:], in1=rs[g][:, 0:1].to_broadcast([P, 512]), op=ALU.mult
                )
            elif on_g:
                nc.gpsimd.tensor_scalar(
                    out=pn[g][:], in0=ex[g][:], scalar1=rs[g][:, 0:1], scalar2=0.0, op0=ALU.mult, op1=ALU.add
                )
            else:
                nc.vector.tensor_scalar(
                    out=pn[g][:], in0=ex[g][:], scalar1=rs[g][:, 0:1], scalar2=None, op0=ALU.mult
                )

        def tr_p(g):
            pair, j = divmod(g, 2)
            if j == 0:
                pt[pair] = psum.tile([P, 1024], BF16, name="pt", tag="pt%d" % (pair % 2))
            for t in range(4):
                nc.tensor.transpose(
                    pt[pair][:, 256 * t + 128 * j : 256 * t + 128 * j + 128],
                    pn[g][:, 128 * t : 128 * t + 128],
                    ident_b[:],
                )

        def cp_p(pair):
            gp[pair] = pq.tile([P, 1024], BF16, name="gp", tag="gp", align_bytes=64)
            nc.scalar.copy(
                out=gp[pair][:].rearrange("p (m t) -> p m t", t=4),
                in_=pt[pair][:].rearrange("p (t m) -> p m t", t=4),
            )

        def quant_p(pair):
            cp[pair] = pq.tile([P, 256], U32, name="cp", tag="cp", align_bytes=64)
            sp[pair] = pq.tile([P, 256], U8, name="sp", tag="sp", align_bytes=64)
            nc.vector.quantize_mx(out=cp[pair][:].bitcast(FP8X4), scales=sp[pair][:], in_=gp[pair][:])

        def pv(g):
            b = g // 4
            pair, j = divmod(g, 2)
            ot[g] = psum.tile([P, 512], F32, name="ot", tag="ot%d" % (g % 2))
            nc.tensor.matmul_mx(
                out=ot[g][:],
                lhsT=cp[pair][:, 128 * j : 128 * j + 128].bitcast(FP8X4),
                lhsT_scale=sp[pair][:, 128 * j : 128 * j + 128],
                rhs=cv[b][:].bitcast(FP8X4),
                rhs_scale=sv[b][:],
                start=True,
                stop=True,
            )

        def cp_o(g, on_vector):
            b, i = divmod(g, 4)
            if i == 0:
                o[b] = opool.tile([P, 4, E], F32, name="o", tag="o")
            if on_vector:
                nc.vector.tensor_copy(out=o[b][:, i, :], in_=ot[g][:])
            else:
                nc.scalar.copy(out=o[b][:, i, :], in_=ot[g][:])
            dst = out[b].rearrange("(p i) e -> p i e", i=4)
            if b == B - 1:
                nc.sync.dma_start(out=dst[:, i, :], in_=o[b][:, i, :])
            elif i % 2 == 1:
                nc.sync.dma_start(out=dst[:, i - 1 : i + 1, :], in_=o[b][:, i - 1 : i + 1, :])

        def okb(b):
            return 0 <= b < B

        def okg(g):
            return 0 <= g < NT

        ctx.enter_context(tc.manual_schedule())

        load_qk(0, 2)
        load_qk(1, 1)
        load_v(0)
        load_qk(2, 1)
        load_v(1)
        load_v(2)
        load_v(3)

        for g in range(-8, NT + 7):
            b, i = divmod(g, 4)
            t5 = g - 6
            o_on_v = t5 >= NT - TAIL_V and i % 2 == 1
            if okg(g + 1):
                vmax(g + 1)
            if okg(g - 1) and g - 1 < NT - 2 and (NORM_ENG[(g - 1) % 4] == "V" or g - 1 >= NT - 8):
                norm(g - 1, False)
            if i == 1 and okb(b + 2):
                cp_q(b + 2, 0)
            if i == 3 and okb(b + 2):
                cp_q(b + 2, 1)
            if i % 2 == 0 and okg(g - 4):
                quant_p((g - 4) // 2)
            if i == 1 and okb(b + 1):
                quant_qk(b + 1)
            if i == 0 and okb(b):
                regroup_v(b)
                if okb(b + 4):
                    load_v(b + 4)
            if i == 2 and okb(b):
                quant_v(b)
            if okg(g):
                vexp(g)
            if okg(g - 1) and g - 1 < NT - 8 and NORM_ENG[(g - 1) % 4] == "S":
                norm(g - 1, False, True)
            if okg(g - 5):
                pv(g - 5)
            if okg(g + 2):
                score(g + 2)
            if okg(g - 1):
                tr_p(g - 1)
            if okb(b + 2):
                trx(b + 2, i // 2, i % 2)
                if i == 3 and okb(b + 5):
                    load_qk(b + 5, 1)
            if i % 2 == 1 and okg(g - 3):
                cp_p((g - 3) // 2)
            if okg(t5) and not o_on_v:
                cp_o(t5, False)
            if i == 2 and okb(b + 2):
                cp_k(b + 2, 0)
            if i == 0 and okb(b + 1):
                cp_k(b + 1, 1)
            if okg(t5) and o_on_v:
                cp_o(t5, True)
            if okg(g):
                if g >= NT - 2:
                    recip(g, False)
                    norm(g, False)
                elif NORM_ENG[i] == "G":
                    recip(g, False)
                    norm(g, True)
                else:
                    recip(g, True)
